import numpy as np
import ml_dtypes


def mxq(x, axis, fmt="e4m3"):
    dtype, down = {"e4m3": (ml_dtypes.float8_e4m3fn, 7), "e5m2": (ml_dtypes.float8_e5m2, 14)}[fmt]
    v = np.moveaxis(np.asarray(x, np.float32).astype(ml_dtypes.bfloat16).astype(np.float64), axis, -1)
    blocks = v.reshape(v.shape[:-1] + (-1, 32))
    amax = np.abs(blocks).max(-1, keepdims=True)
    byte = np.maximum(np.where(amax > 0, np.frexp(amax)[1] - 1 + 127, 0) - down, 1)
    scale = np.exp2(byte - 127.0)
    codes = (blocks / scale).astype(np.float32).astype(dtype).astype(np.float64)
    return np.moveaxis((codes * scale).reshape(v.shape), -1, axis)


WIDE = False


def mx_kscale(k):
    if not WIDE:
        return np.ones(k)
    levels = np.array([20, -20, 10, -10, 0])
    a = np.random.permutation(np.resize(levels, k // 512 * 4)).reshape(k // 512, 4)
    idx = np.arange(k)
    return np.exp2(a[idx // 512, idx % 128 // 32])


BF16 = ml_dtypes.bfloat16


def bf(x):
    return np.asarray(x, np.float32).astype(BF16)


def f64(x):
    return np.asarray(x).astype(np.float64)


B, I, C, L, O, KW, P = 2, 1024, 2, 512, 512, 3, 1


def setup_inputs():
    u = mx_kscale(O)
    x = np.random.standard_normal((B, I, C, L))
    t = np.random.uniform(0.0, 1.0, (B, C, L))
    w = np.random.standard_normal((O, I, C, KW)) / np.sqrt(I * KW) / u[:, None, None, None]
    g = (np.random.standard_normal((B, O, C, L)) * np.exp2(np.random.randint(-12, 1, (B, 1, C, L)))
         * 16.0 * u[None, :, None, None])
    return {"x": bf(x), "time_tensor": bf(t), "weights": bf(w), "grad_out": bf(g)}


def reference(x, time_tensor, weights, grad_out):
    gq = mxq(f64(grad_out).transpose(0, 2, 1, 3), 2, "e5m2")
    wt = f64(weights).transpose(3, 2, 1, 0)
    t = f64(time_tensor)[:, :, None, :]
    gx = np.zeros((B, C, I, L))
    for j in range(KW):
        z = (mxq(wt[j], 2, "e4m3") @ gq) * t
        zp = np.pad(z, ((0, 0), (0, 0), (0, 0), (P, P)))
        gx = gx + zp[..., 2 * P - j:2 * P - j + L]
    return np.transpose(gx, (0, 2, 1, 3))

@@ -1,0 +1,298 @@
+from contextlib import ExitStack
+
+import concourse.mybir as mybir
+from concourse.masks import make_identity
+
+F32 = mybir.dt.float32
+BF16 = mybir.dt.bfloat16
+U32 = mybir.dt.uint32
+U8 = mybir.dt.uint8
+E4 = mybir.dt.float8_e4m3fn_x4
+E5 = mybir.dt.float8_e5m2_x4
+MULT = mybir.AluOpType.mult
+ADD = mybir.AluOpType.add
+COPY = mybir.ActivationFunctionType.Copy
+
+P = 128
+B, I, C, L, O, KW = 2, 1024, 2, 512, 512, 3
+PACK = 4
+NH = 2
+IH = I // NH
+NA = L // 4
+FLOPS = 2 * B * C * KW * I * O * L
+BYTES = 2 * (O * I * C * KW + B * O * C * L + B * C * L) + 4 * B * I * C * L
+
+PIN = False
+W_PIECES = (((0, 256), (256, 384), (384, 512)), ((0, 256), (256, 512)))
+N_TILES = 32
+NZS = 2
+NZV = 4
+NACC = 12
+NOSB = 2
+TXQ = 2
+LATE_S = (0, 2, 4, 6, 10)
+HEAD = (
+    ("rg", "v", 0), ("xg", 0), ("qg", 0), ("tt",),
+    ("rw", "v", 0, 0, 0, 172), ("rw", "s", 0, 0, 172, 256), ("rw", "s", 0, 1, 0, 64), ("qw", 0, 0, 0, 256),
+    ("rw", "v", 0, 0, 256, 340), ("rw", "s", 0, 0, 340, 384), ("rw", "s", 0, 1, 64, 160), ("qw", 0, 0, 256, 384),
+    ("rw", "v", 0, 0, 384, 468), ("rw", "s", 0, 0, 468, 512), ("qw", 0, 0, 384, 512),
+)
+
+
+def make_fill():
+    fill = {0: [("rw", "s", 0, 1, 160, 256), ("rg", "v", 2), ("rw", "s", 0, 1, 256, 384), ("xg", 2), ("qg", 2)],
+            1: [("rg", "s", 1), ("qw", 0, 1, 0, 256), ("rw", "s", 0, 1, 384, 512), ("xg", 1), ("qg", 1)],
+            2: [("qw", 0, 1, 256, 384), ("qw", 0, 1, 384, 512), ("rg", "s", 3)],
+            3: [("xg", 3), ("qg", 3)]}
+    for c in range(C):
+        for k in range(4):
+            q = 2 + 4 * c + k
+            fill[q] = fill.get(q, []) + [("rw", "s", 1, c, 128 * k, 128 * k + 80), ("rw", "v", 1, c, 128 * k + 80, 128 * k + 128)]
+        fill[5 + 4 * c] = fill.get(5 + 4 * c, []) + [("qw", 1, c, 0, 256)]
+        fill[6 + 4 * c] = [("qw", 1, c, 256, 512)] + fill.get(6 + 4 * c, [])
+    return fill
+
+
+FILL = make_fill()
+
+
+def tile_timeawareconv1d_t_kernel(tc, x, time_tensor, weights, grad_out, out):
+    nc = tc.nc
+    with ExitStack() as ctx:
+        keep = ctx.enter_context(tc.tile_pool(name="keep", bufs=1))
+        psum = ctx.enter_context(tc.psum_pool(name="psum", bufs=1))
+        if PIN:
+            ctx.enter_context(tc.manual_schedule())
+
+        ident = keep.tile([P, P], F32, name="ident")
+        zb = keep.tile([P, P + 2], BF16, name="zb")
+        tmain = keep.tile([P, 32], BF16, name="tmain")
+        tt = keep.tile([P, 3, 16], F32, name="tt")
+        graw = [keep.tile([P, PACK, L], BF16, name="graw%d" % g) for g in range(4)]
+        gg = [keep.tile([P, 6, NA, PACK], BF16, name="gg%d" % g, align_bytes=64) for g in range(4)]
+        gq = [keep.tile([P, 6 * NA], U32, name="gq%d" % g, align_bytes=64) for g in range(4)]
+        gs = [keep.tile([P, 6 * NA], U8, name="gs%d" % g, align_bytes=64) for g in range(4)]
+        wraw = [
+            [keep.tile([P, PACK, (q1 - q0) * C * KW], BF16, name="wraw%d_%d" % (h, q0)) for (q0, q1) in W_PIECES[h]]
+            for h in range(NH)
+        ]
+        wg = [[keep.tile([P, KW, IH, PACK], BF16, name="wg%d%d" % (h, c), align_bytes=64) for c in range(C)] for h in range(NH)]
+        wq = [[keep.tile([P, KW, IH], U32, name="wq%d%d" % (h, c), align_bytes=64) for c in range(C)] for h in range(NH)]
+        ws = [[keep.tile([P, KW, IH], U8, name="ws%d%d" % (h, c), align_bytes=64) for c in range(C)] for h in range(NH)]
+
+        nc.vector.memset(tmain[:], 0.0)
+        nc.scalar.dma_start(
+            out=tmain[:, 0:16].rearrange("p (g r) -> p g r", r=4),
+            in_=time_tensor.rearrange("b c (a r) -> a (b c) r", r=4),
+        )
+
+        def load_g(g):
+            nc.sync.dma_start(out=graw[g][:], in_=grad_out[g // 2, :, g % 2, :].rearrange("(p t) l -> p t l", t=PACK))
+
+        wview = weights.rearrange("(p t) i c j -> p t (i c j)", t=PACK)
+
+        def load_w(h):
+            for (q0, q1), raw in zip(W_PIECES[h], wraw[h]):
+                nc.sync.dma_start(out=raw[:], in_=wview[:, :, (h * IH + q0) * C * KW:(h * IH + q1) * C * KW])
+
+        load_g(0)
+        load_w(0)
+        load_g(2)
+        load_g(1)
+        load_g(3)
+        load_w(1)
+
+        make_identity(nc, ident[:])
+        nc.gpsimd.memset(zb[:], 0.0)
+        make_identity(nc, zb[:, 1:P + 1], nomemset=True)
+        for g in range(4):
+            nc.vector.memset(gg[g][:, 0, 0, :], 0.0)
+            nc.vector.memset(gg[g][:, 5, NA - 1, :], 0.0)
+
+        def copy(eng, dst, src):
+            if eng == "v":
+                nc.vector.tensor_copy(out=dst, in_=src)
+            elif eng == "s":
+                nc.scalar.copy(out=dst, in_=src)
+            else:
+                nc.gpsimd.tensor_scalar(out=dst, in0=src, scalar1=1.0, scalar2=0.0, op0=MULT, op1=ADD)
+
+        def rg(eng, g):
+            copy(eng, gg[g][:, 1:5, :, :].rearrange("p r a t -> p a t r"),
+                 graw[g][:].rearrange("p t (a r) -> p a t r", r=4))
+
+        def xg(g):
+            nc.vector.tensor_copy(out=gg[g][:, 0, 1:NA, :], in_=gg[g][:, 4, 0:NA - 1, :])
+            nc.vector.tensor_copy(out=gg[g][:, 5, 0:NA - 1, :], in_=gg[g][:, 1, 1:NA, :])
+
+        ready = set()
+        rcnt = {}
+
+        def qg(g):
+            ready.add(("g", g))
+            flat = gg[g][:].rearrange("p k a t -> p (k a t)")
+            for (c0, c1) in ((0, 2048), (2048, 3072)):
+                nc.vector.quantize_mx(out=gq[g][:, c0 // 4:c1 // 4].bitcast(E5), scales=gs[g][:, c0 // 4:c1 // 4],
+                                      in_=flat[:, c0:c1])
+
+        def rw(eng, h, c, i0, i1):
+            for i in range(i0, i1, 4):
+                rcnt[(h, c, i // 64)] = rcnt.get((h, c, i // 64), 0) + 1
+                if rcnt[(h, c, i // 64)] == 16:
+                    ready.add(("r", h, c, i // 64 * 64))
+            for (q0, q1), raw in zip(W_PIECES[h], wraw[h]):
+                if q0 <= i0 and i1 <= q1:
+                    src = raw[:].rearrange("p t (i c j) -> p i t c j", c=C, j=KW)[:, i0 - q0:i1 - q0, :, c, :]
+                    copy(eng, wg[h][c][:, :, i0:i1, :].rearrange("p j i t -> p i t j"), src)
+
+        def qw(h, c, i0, i1):
+            for i in range(i0, i1, 64):
+                assert ("r", h, c, i) in ready, (h, c, i)
+                ready.add(("w", h, c, i))
+            for j in (1, 0, 2):
+                nc.vector.quantize_mx(out=wq[h][c][:, j, i0:i1].bitcast(E4), scales=ws[h][c][:, j, i0:i1],
+                                      in_=wg[h][c][:, j, i0:i1, :].rearrange("p i t -> p (i t)"))
+
+        def ttable():
+            tps = psum.tile([P, 2, 32], F32, tag="t0", name="tps")
+            nc.tensor.matmul(out=tps[:, 0, :], lhsT=zb[:, 0:P], rhs=tmain[:], start=True, stop=True)
+            nc.tensor.matmul(out=tps[:, 1, :], lhsT=zb[:, 2:P + 2], rhs=tmain[:], start=True, stop=True)
+            nc.vector.tensor_copy(out=tt[:, 0:2, :], in_=tps[:, :, 0:16])
+            nc.vector.tensor_copy(out=tt[:, 2, :], in_=tmain[:, 0:16])
+
+        def tscal(g, r, j):
+            rr = r + 1 - j
+            if rr < 0:
+                return tt[:, 0, g * 4 + 3:g * 4 + 4]
+            if rr > 3:
+                return tt[:, 1, g * 4:g * 4 + 1]
+            return tt[:, 2, g * 4 + rr:g * 4 + rr + 1]
+
+        def unit(u):
+            return u // 4, (u // 2) % 2, u % 2
+
+        zt = {}
+        acc = {}
+        tp = {}
+        osb = {}
+
+        def mx_pass(n, j):
+            h, c, b = unit(n // 4)
+            g = b * 2 + c
+            assert ("g", g) in ready, n
+            assert all(("w", h, c, i) in ready for i in range(0, IH, 64)), n
+            if j == 1:
+                tag = "zs%d" % (n % NZS)
+            else:
+                tag = "zv%d" % ((2 * n + j // 2) % NZV)
+            z = psum.tile([P, IH], F32, tag=tag, name="z%d_%d" % (n, j))
+            zt[(n, j)] = z
+            blk = n % 4 + 2 - j
+            nc.tensor.matmul_mx(out=z[:], lhsT=gq[g][:, blk * NA:(blk + 1) * NA].bitcast(E5),
+                                lhsT_scale=gs[g][:, blk * NA:(blk + 1) * NA],
+                                rhs=wq[h][c][:, j, :].bitcast(E4), rhs_scale=ws[h][c][:, j, :],
+                                start=True, stop=True)
+
+        def zexit(n):
+            h, c, b = unit(n // 4)
+            a = keep.tile([P, IH], F32, tag="acc%d" % (n % NACC), name="acc_%d" % n)
+            acc[n] = a
+            nc.scalar.activation(out=a[:], in_=zt[(n, 1)][:], func=COPY, scale=tscal(b * 2 + c, n % 4, 1))
+
+        def fused(n, j):
+            h, c, b = unit(n // 4)
+            nc.vector.scalar_tensor_tensor(out=acc[n][:], in0=zt[(n, j)][:], scalar=tscal(b * 2 + c, n % 4, j),
+                                           in1=acc[n][:], op0=MULT, op1=ADD)
+
+        def tr(k, tag):
+            u, ib = k // 4, k % 4
+            t = psum.tile([P, 4, NA], F32, tag=tag, name="tp%d_%d" % (u, ib))
+            tp[k] = t
+            for r in range(4):
+                nc.tensor.transpose(out=t[:, r, :], in_=acc[4 * u + r][:, ib * P:(ib + 1) * P], identity=ident[:])
+
+        def texit(eng, k):
+            u, ib = k // 4, k % 4
+            if ib == 0:
+                osb[u] = keep.tile([P, 4, L], F32, tag="osb%d" % (u % NOSB), name="osb_%d" % u)
+            copy(eng, osb[u][:, ib, :].rearrange("p (a r) -> p a r", r=4), tp[k][:].rearrange("p r a -> p a r"))
+
+        def store(u, k0, k1):
+            h, c, b = unit(u)
+            nc.sync.dma_start(
+                out=out[b, h * IH + k0 * P:h * IH + k1 * P, c, :].rearrange("(k p) m -> p k m", p=P),
+                in_=osb[u][:, k0:k1, :],
+            )
+
+        def do(f):
+            if f[0] == "rg":
+                rg(f[1], f[2])
+            elif f[0] == "xg":
+                xg(f[1])
+            elif f[0] == "qg":
+                qg(f[1])
+            elif f[0] == "qw":
+                qw(f[1], f[2], f[3], f[4])
+            else:
+                rw(f[1], f[2], f[3], f[4], f[5])
+
+        for f in HEAD:
+            if f[0] == "tt":
+                ttable()
+            else:
+                do(f)
+        for j in (1, 0, 2):
+            mx_pass(0, j)
+            mx_pass(1, j)
+        for n in range(2):
+            zexit(n)
+        for n in range(2):
+            mx_pass(n + 2, 1)
+
+        NQ = N_TILES // 2
+        for q in range(NQ):
+            ta, tb = 2 * q, 2 * q + 1
+            for f in FILL.get(q, []):
+                if f[0] == "pre":
+                    do(f[1:])
+            if q + 1 < NQ:
+                zexit(ta + 2)
+                zexit(tb + 2)
+            for j in (0, 2):
+                fused(ta, j)
+                fused(tb, j)
+            for f in FILL.get(q, []):
+                if f[0] == "mid":
+                    do(f[1:])
+            k = 2 * (q - TXQ)
+            if 0 <= k < 28:
+                texit("s", k)
+                texit("s", k + 1)
+                if k % 4 == 2:
+                    store(k // 4, 0, 4)
+            if q + 2 < NQ and q not in LATE_S:
+                mx_pass(ta + 4, 1)
+                mx_pass(tb + 4, 1)
+            if q + 1 < NQ:
+                for j in (0, 2):
+                    mx_pass(ta + 2, j)
+                    mx_pass(tb + 2, j)
+            if q >= 1 and q < NQ - 1:
+                tr(2 * q - 2, "t0")
+                tr(2 * q - 1, "t1")
+            for f in FILL.get(q, []):
+                if f[0] != "pre" and f[0] != "mid":
+                    do(f)
+            if q + 2 < NQ and q in LATE_S:
+                mx_pass(ta + 4, 1)
+                mx_pass(tb + 4, 1)
+        tr(28, "t0")
+        tr(29, "t1")
+        tr(30, "zv0")
+        tr(31, "zv1")
+        texit("s", 28)
+        texit("v", 29)
+        store(7, 0, 2)
+        texit("s", 30)
+        texit("v", 31)
+        store(7, 2, 4)

@@ -23,7 +23,7 @@ FLOPS = 2 * B * C * KW * I * O * L
 BYTES = 2 * (O * I * C * KW + B * O * C * L + B * C * L) + 4 * B * I * C * L
 
 PIN = False
-W_PIECES = (((0, 256), (256, 384), (384, 512)), ((0, 256), (256, 512)))
+W_PIECES = (((0, 128), (128, 256), (256, 384), (384, 512)), ((0, 256), (256, 512)))
 N_TILES = 32
 NZS = 2
 NZV = 4
@@ -32,17 +32,18 @@ NOSB = 2
 TXQ = 2
 LATE_S = (0, 2, 4, 6, 10)
 HEAD = (
-    ("rg", "v", 0), ("xg", 0), ("qg", 0), ("tt",),
-    ("rw", "v", 0, 0, 0, 172), ("rw", "s", 0, 0, 172, 256), ("rw", "s", 0, 1, 0, 64), ("qw", 0, 0, 0, 256),
-    ("rw", "v", 0, 0, 256, 340), ("rw", "s", 0, 0, 340, 384), ("rw", "s", 0, 1, 64, 160), ("qw", 0, 0, 256, 384),
-    ("rw", "v", 0, 0, 384, 468), ("rw", "s", 0, 0, 468, 512), ("qw", 0, 0, 384, 512),
+    ("rg", "v", 0, 0, 64), ("rg", "s", 0, 64, 128), ("xg", 0), ("qg", 0), ("tt",),
+    ("rw", "v", 0, 0, 0, 76), ("rw", "s", 0, 0, 76, 128),
+    ("rw", "v", 0, 0, 128, 204), ("rw", "s", 0, 0, 204, 256), ("qw", 0, 0, 0, 256),
+    ("rw", "v", 0, 0, 256, 332), ("rw", "s", 0, 0, 332, 384), ("qw", 0, 0, 256, 384),
+    ("rw", "v", 0, 0, 384, 460), ("rw", "s", 0, 0, 460, 512), ("qw", 0, 0, 384, 512),
 )
 
 
 def make_fill():
-    fill = {0: [("rw", "s", 0, 1, 160, 256), ("rg", "v", 2), ("rw", "s", 0, 1, 256, 384), ("xg", 2), ("qg", 2)],
-            1: [("rg", "s", 1), ("qw", 0, 1, 0, 256), ("rw", "s", 0, 1, 384, 512), ("xg", 1), ("qg", 1)],
-            2: [("qw", 0, 1, 256, 384), ("qw", 0, 1, 384, 512), ("rg", "s", 3)],
+    fill = {0: [("rw", "s", 0, 1, 0, 256), ("rg", "v", 2, 0, NA), ("rw", "s", 0, 1, 256, 384), ("xg", 2), ("qg", 2)],
+            1: [("rg", "s", 1, 0, NA), ("qw", 0, 1, 0, 256), ("rw", "s", 0, 1, 384, 512), ("xg", 1), ("qg", 1)],
+            2: [("qw", 0, 1, 256, 384), ("qw", 0, 1, 384, 512), ("rg", "s", 3, 0, NA)],
             3: [("xg", 3), ("qg", 3)]}
     for c in range(C):
         for k in range(4):
@@ -81,7 +82,7 @@ def tile_timeawareconv1d_t_kernel(tc, x, time_tensor, weights, grad_out, out):
         ws = [[keep.tile([P, KW, IH], U8, name="ws%d%d" % (h, c), align_bytes=64) for c in range(C)] for h in range(NH)]
 
         nc.vector.memset(tmain[:], 0.0)
-        nc.scalar.dma_start(
+        nc.sync.dma_start(
             out=tmain[:, 0:16].rearrange("p (g r) -> p g r", r=4),
             in_=time_tensor.rearrange("b c (a r) -> a (b c) r", r=4),
         )
@@ -117,9 +118,9 @@ def tile_timeawareconv1d_t_kernel(tc, x, time_tensor, weights, grad_out, out):
             else:
                 nc.gpsimd.tensor_scalar(out=dst, in0=src, scalar1=1.0, scalar2=0.0, op0=MULT, op1=ADD)
 
-        def rg(eng, g):
-            copy(eng, gg[g][:, 1:5, :, :].rearrange("p r a t -> p a t r"),
-                 graw[g][:].rearrange("p t (a r) -> p a t r", r=4))
+        def rg(eng, g, a0, a1):
+            copy(eng, gg[g][:, 1:5, a0:a1, :].rearrange("p r a t -> p a t r"),
+                 graw[g][:].rearrange("p t (a r) -> p a t r", r=4)[:, a0:a1, :, :])
 
         def xg(g):
             nc.vector.tensor_copy(out=gg[g][:, 0, 1:NA, :], in_=gg[g][:, 4, 0:NA - 1, :])
@@ -141,9 +142,10 @@ def tile_timeawareconv1d_t_kernel(tc, x, time_tensor, weights, grad_out, out):
                 if rcnt[(h, c, i // 64)] == 16:
                     ready.add(("r", h, c, i // 64 * 64))
             for (q0, q1), raw in zip(W_PIECES[h], wraw[h]):
-                if q0 <= i0 and i1 <= q1:
-                    src = raw[:].rearrange("p t (i c j) -> p i t c j", c=C, j=KW)[:, i0 - q0:i1 - q0, :, c, :]
-                    copy(eng, wg[h][c][:, :, i0:i1, :].rearrange("p j i t -> p i t j"), src)
+                e0, e1 = max(i0, q0), min(i1, q1)
+                if e0 < e1:
+                    src = raw[:].rearrange("p t (i c j) -> p i t c j", c=C, j=KW)[:, e0 - q0:e1 - q0, :, c, :]
+                    copy(eng, wg[h][c][:, :, e0:e1, :].rearrange("p j i t -> p i t j"), src)
 
         def qw(h, c, i0, i1):
             for i in range(i0, i1, 64):
@@ -226,7 +228,7 @@ def tile_timeawareconv1d_t_kernel(tc, x, time_tensor, weights, grad_out, out):
 
         def do(f):
             if f[0] == "rg":
-                rg(f[1], f[2])
+                rg(f[1], f[2], f[3], f[4])
             elif f[0] == "xg":
                 xg(f[1])
             elif f[0] == "qg":

@@ -68,6 +68,7 @@ def tile_timeawareconv1d_t_kernel(tc, x, time_tensor, weights, grad_out, out):
         ident = keep.tile([P, P], F32, name="ident")
         zb = keep.tile([P, P + 2], BF16, name="zb")
         tmain = keep.tile([P, 32], BF16, name="tmain")
+        trow = keep.tile([P, L], BF16, name="trow")
         tt = keep.tile([P, 3, 16], F32, name="tt")
         graw = [keep.tile([P, PACK, L], BF16, name="graw%d" % g) for g in range(4)]
         gg = [keep.tile([P, 6, NA, PACK], BF16, name="gg%d" % g, align_bytes=64) for g in range(4)]
@@ -82,10 +83,8 @@ def tile_timeawareconv1d_t_kernel(tc, x, time_tensor, weights, grad_out, out):
         ws = [[keep.tile([P, KW, IH], U8, name="ws%d%d" % (h, c), align_bytes=64) for c in range(C)] for h in range(NH)]
 
         nc.vector.memset(tmain[:], 0.0)
-        nc.sync.dma_start(
-            out=tmain[:, 0:16].rearrange("p (g r) -> p g r", r=4),
-            in_=time_tensor.rearrange("b c (a r) -> a (b c) r", r=4),
-        )
+        nc.vector.memset(trow[:], 0.0)
+        nc.sync.dma_start(out=trow[0:4, :], in_=time_tensor.rearrange("b c l -> (b c) l"))
 
         def load_g(g):
             nc.sync.dma_start(out=graw[g][:], in_=grad_out[g // 2, :, g % 2, :].rearrange("(p t) l -> p t l", t=PACK))
@@ -156,6 +155,12 @@ def tile_timeawareconv1d_t_kernel(tc, x, time_tensor, weights, grad_out, out):
                                       in_=wg[h][c][:, j, i0:i1, :].rearrange("p i t -> p (i t)"))
 
         def ttable():
+            tcol = psum.tile([P, 4, P], BF16, tag="t1", name="tcol")
+            for r in range(4):
+                nc.tensor.transpose(out=tcol[:, r, :], in_=trow[:].rearrange("p (a r) -> p a r", r=4)[:, :, r],
+                                    identity=zb[:, 1:P + 1])
+            nc.vector.tensor_copy(out=tmain[:, 0:16].rearrange("p (g r) -> p g r", r=4),
+                                  in_=tcol[:, :, 0:4].rearrange("p r g -> p g r"))
             tps = psum.tile([P, 2, 32], F32, tag="t0", name="tps")
             nc.tensor.matmul(out=tps[:, 0, :], lhsT=zb[:, 0:P], rhs=tmain[:], start=True, stop=True)
             nc.tensor.matmul(out=tps[:, 1, :], lhsT=zb[:, 2:P + 2], rhs=tmain[:], start=True, stop=True)

from contextlib import ExitStack

import concourse.mybir as mybir
from concourse.masks import make_identity

F32 = mybir.dt.float32
BF16 = mybir.dt.bfloat16
U32 = mybir.dt.uint32
U8 = mybir.dt.uint8
E4 = mybir.dt.float8_e4m3fn_x4
E5 = mybir.dt.float8_e5m2_x4
MULT = mybir.AluOpType.mult
ADD = mybir.AluOpType.add
COPY = mybir.ActivationFunctionType.Copy

P = 128
B, I, C, L, O, KW = 2, 1024, 2, 512, 512, 3
PACK = 4
NH = 2
IH = I // NH
NA = L // 4
FLOPS = 2 * B * C * KW * I * O * L
BYTES = 2 * (O * I * C * KW + B * O * C * L + B * C * L) + 4 * B * I * C * L

PIN = False
W_PIECES = (((0, 128), (128, 256), (256, 384), (384, 512)), ((0, 256), (256, 512)))
N_TILES = 32
NZS = 2
NZV = 4
NACC = 12
NOSB = 2
TXQ = 2
LATE_S = (0, 2, 4, 6, 10)
HEAD = (
    ("rg", "v", 0, 0, 64), ("rg", "s", 0, 64, 128), ("xg", 0), ("qg", 0), ("tt",),
    ("rw", "v", 0, 0, 0, 76), ("rw", "s", 0, 0, 76, 128),
    ("rw", "v", 0, 0, 128, 204), ("rw", "s", 0, 0, 204, 256), ("qw", 0, 0, 0, 256),
    ("rw", "v", 0, 0, 256, 332), ("rw", "s", 0, 0, 332, 384), ("qw", 0, 0, 256, 384),
    ("rw", "v", 0, 0, 384, 460), ("rw", "s", 0, 0, 460, 512), ("qw", 0, 0, 384, 512),
)


def make_fill():
    fill = {0: [("rw", "s", 0, 1, 0, 256), ("rg", "v", 2, 0, NA), ("rw", "s", 0, 1, 256, 384), ("xg", 2), ("qg", 2)],
            1: [("rg", "s", 1, 0, NA), ("qw", 0, 1, 0, 256), ("rw", "s", 0, 1, 384, 512), ("xg", 1), ("qg", 1)],
            2: [("qw", 0, 1, 256, 384), ("qw", 0, 1, 384, 512), ("rg", "s", 3, 0, NA)],
            3: [("xg", 3), ("qg", 3)]}
    for c in range(C):
        for k in range(4):
            q = 2 + 4 * c + k
            fill[q] = fill.get(q, []) + [("rw", "s", 1, c, 128 * k, 128 * k + 80), ("rw", "v", 1, c, 128 * k + 80, 128 * k + 128)]
        fill[5 + 4 * c] = fill.get(5 + 4 * c, []) + [("qw", 1, c, 0, 256)]
        fill[6 + 4 * c] = [("qw", 1, c, 256, 512)] + fill.get(6 + 4 * c, [])
    return fill


FILL = make_fill()


def tile_timeawareconv1d_t_kernel(tc, x, time_tensor, weights, grad_out, out):
    nc = tc.nc
    with ExitStack() as ctx:
        keep = ctx.enter_context(tc.tile_pool(name="keep", bufs=1))
        psum = ctx.enter_context(tc.psum_pool(name="psum", bufs=1))
        if PIN:
            ctx.enter_context(tc.manual_schedule())

        ident = keep.tile([P, P], F32, name="ident")
        zb = keep.tile([P, P + 2], BF16, name="zb")
        tmain = keep.tile([P, 32], BF16, name="tmain")
        trow = keep.tile([P, L], BF16, name="trow")
        tt = keep.tile([P, 3, 16], F32, name="tt")
        graw = [keep.tile([P, PACK, L], BF16, name="graw%d" % g) for g in range(4)]
        gg = [keep.tile([P, 6, NA, PACK], BF16, name="gg%d" % g, align_bytes=64) for g in range(4)]
        gq = [keep.tile([P, 6 * NA], U32, name="gq%d" % g, align_bytes=64) for g in range(4)]
        gs = [keep.tile([P, 6 * NA], U8, name="gs%d" % g, align_bytes=64) for g in range(4)]
        wraw = [
            [keep.tile([P, PACK, (q1 - q0) * C * KW], BF16, name="wraw%d_%d" % (h, q0)) for (q0, q1) in W_PIECES[h]]
            for h in range(NH)
        ]
        wg = [[keep.tile([P, KW, IH, PACK], BF16, name="wg%d%d" % (h, c), align_bytes=64) for c in range(C)] for h in range(NH)]
        wq = [[keep.tile([P, KW, IH], U32, name="wq%d%d" % (h, c), align_bytes=64) for c in range(C)] for h in range(NH)]
        ws = [[keep.tile([P, KW, IH], U8, name="ws%d%d" % (h, c), align_bytes=64) for c in range(C)] for h in range(NH)]

        nc.vector.memset(tmain[:], 0.0)
        nc.vector.memset(trow[:], 0.0)
        nc.sync.dma_start(out=trow[0:4, :], in_=time_tensor.rearrange("b c l -> (b c) l"))

        def load_g(g):
            nc.sync.dma_start(out=graw[g][:], in_=grad_out[g // 2, :, g % 2, :].rearrange("(p t) l -> p t l", t=PACK))

        wview = weights.rearrange("(p t) i c j -> p t (i c j)", t=PACK)

        def load_w(h):
            for (q0, q1), raw in zip(W_PIECES[h], wraw[h]):
                nc.sync.dma_start(out=raw[:], in_=wview[:, :, (h * IH + q0) * C * KW:(h * IH + q1) * C * KW])

        load_g(0)
        load_w(0)
        load_g(2)
        load_g(1)
        load_g(3)
        load_w(1)

        make_identity(nc, ident[:])
        nc.gpsimd.memset(zb[:], 0.0)
        make_identity(nc, zb[:, 1:P + 1], nomemset=True)
        for g in range(4):
            nc.vector.memset(gg[g][:, 0, 0, :], 0.0)
            nc.vector.memset(gg[g][:, 5, NA - 1, :], 0.0)

        def copy(eng, dst, src):
            if eng == "v":
                nc.vector.tensor_copy(out=dst, in_=src)
            elif eng == "s":
                nc.scalar.copy(out=dst, in_=src)
            else:
                nc.gpsimd.tensor_scalar(out=dst, in0=src, scalar1=1.0, scalar2=0.0, op0=MULT, op1=ADD)

        def rg(eng, g, a0, a1):
            copy(eng, gg[g][:, 1:5, a0:a1, :].rearrange("p r a t -> p a t r"),
                 graw[g][:].rearrange("p t (a r) -> p a t r", r=4)[:, a0:a1, :, :])

        def xg(g):
            nc.vector.tensor_copy(out=gg[g][:, 0, 1:NA, :], in_=gg[g][:, 4, 0:NA - 1, :])
            nc.vector.tensor_copy(out=gg[g][:, 5, 0:NA - 1, :], in_=gg[g][:, 1, 1:NA, :])

        ready = set()
        rcnt = {}

        def qg(g):
            ready.add(("g", g))
            flat = gg[g][:].rearrange("p k a t -> p (k a t)")
            for (c0, c1) in ((0, 2048), (2048, 3072)):
                nc.vector.quantize_mx(out=gq[g][:, c0 // 4:c1 // 4].bitcast(E5), scales=gs[g][:, c0 // 4:c1 // 4],
                                      in_=flat[:, c0:c1])

        def rw(eng, h, c, i0, i1):
            for i in range(i0, i1, 4):
                rcnt[(h, c, i // 64)] = rcnt.get((h, c, i // 64), 0) + 1
                if rcnt[(h, c, i // 64)] == 16:
                    ready.add(("r", h, c, i // 64 * 64))
            for (q0, q1), raw in zip(W_PIECES[h], wraw[h]):
                e0, e1 = max(i0, q0), min(i1, q1)
                if e0 < e1:
                    src = raw[:].rearrange("p t (i c j) -> p i t c j", c=C, j=KW)[:, e0 - q0:e1 - q0, :, c, :]
                    copy(eng, wg[h][c][:, :, e0:e1, :].rearrange("p j i t -> p i t j"), src)

        def qw(h, c, i0, i1):
            for i in range(i0, i1, 64):
                assert ("r", h, c, i) in ready, (h, c, i)
                ready.add(("w", h, c, i))
            for j in (1, 0, 2):
                nc.vector.quantize_mx(out=wq[h][c][:, j, i0:i1].bitcast(E4), scales=ws[h][c][:, j, i0:i1],
                                      in_=wg[h][c][:, j, i0:i1, :].rearrange("p i t -> p (i t)"))

        def ttable():
            tcol = psum.tile([P, 4, P], BF16, tag="t1", name="tcol")
            for r in range(4):
                nc.tensor.transpose(out=tcol[:, r, :], in_=trow[:].rearrange("p (a r) -> p a r", r=4)[:, :, r],
                                    identity=zb[:, 1:P + 1])
            nc.vector.tensor_copy(out=tmain[:, 0:16].rearrange("p (g r) -> p g r", r=4),
                                  in_=tcol[:, :, 0:4].rearrange("p r g -> p g r"))
            tps = psum.tile([P, 2, 32], F32, tag="t0", name="tps")
            nc.tensor.matmul(out=tps[:, 0, :], lhsT=zb[:, 0:P], rhs=tmain[:], start=True, stop=True)
            nc.tensor.matmul(out=tps[:, 1, :], lhsT=zb[:, 2:P + 2], rhs=tmain[:], start=True, stop=True)
            nc.vector.tensor_copy(out=tt[:, 0:2, :], in_=tps[:, :, 0:16])
            nc.vector.tensor_copy(out=tt[:, 2, :], in_=tmain[:, 0:16])

        def tscal(g, r, j):
            rr = r + 1 - j
            if rr < 0:
                return tt[:, 0, g * 4 + 3:g * 4 + 4]
            if rr > 3:
                return tt[:, 1, g * 4:g * 4 + 1]
            return tt[:, 2, g * 4 + rr:g * 4 + rr + 1]

        def unit(u):
            return u // 4, (u // 2) % 2, u % 2

        zt = {}
        acc = {}
        tp = {}
        osb = {}

        def mx_pass(n, j):
            h, c, b = unit(n // 4)
            g = b * 2 + c
            assert ("g", g) in ready, n
            assert all(("w", h, c, i) in ready for i in range(0, IH, 64)), n
            if j == 1:
                tag = "zs%d" % (n % NZS)
            else:
                tag = "zv%d" % ((2 * n + j // 2) % NZV)
            z = psum.tile([P, IH], F32, tag=tag, name="z%d_%d" % (n, j))
            zt[(n, j)] = z
            blk = n % 4 + 2 - j
            nc.tensor.matmul_mx(out=z[:], lhsT=gq[g][:, blk * NA:(blk + 1) * NA].bitcast(E5),
                                lhsT_scale=gs[g][:, blk * NA:(blk + 1) * NA],
                                rhs=wq[h][c][:, j, :].bitcast(E4), rhs_scale=ws[h][c][:, j, :],
                                start=True, stop=True)

        def zexit(n):
            h, c, b = unit(n // 4)
            a = keep.tile([P, IH], F32, tag="acc%d" % (n % NACC), name="acc_%d" % n)
            acc[n] = a
            nc.scalar.activation(out=a[:], in_=zt[(n, 1)][:], func=COPY, scale=tscal(b * 2 + c, n % 4, 1))

        def fused(n, j):
            h, c, b = unit(n // 4)
            nc.vector.scalar_tensor_tensor(out=acc[n][:], in0=zt[(n, j)][:], scalar=tscal(b * 2 + c, n % 4, j),
                                           in1=acc[n][:], op0=MULT, op1=ADD)

        def tr(k, tag):
            u, ib = k // 4, k % 4
            t = psum.tile([P, 4, NA], F32, tag=tag, name="tp%d_%d" % (u, ib))
            tp[k] = t
            for r in range(4):
                nc.tensor.transpose(out=t[:, r, :], in_=acc[4 * u + r][:, ib * P:(ib + 1) * P], identity=ident[:])

        def texit(eng, k):
            u, ib = k // 4, k % 4
            if ib == 0:
                osb[u] = keep.tile([P, 4, L], F32, tag="osb%d" % (u % NOSB), name="osb_%d" % u)
            copy(eng, osb[u][:, ib, :].rearrange("p (a r) -> p a r", r=4), tp[k][:].rearrange("p r a -> p a r"))

        def store(u, k0, k1):
            h, c, b = unit(u)
            nc.sync.dma_start(
                out=out[b, h * IH + k0 * P:h * IH + k1 * P, c, :].rearrange("(k p) m -> p k m", p=P),
                in_=osb[u][:, k0:k1, :],
            )

        def do(f):
            if f[0] == "rg":
                rg(f[1], f[2], f[3], f[4])
            elif f[0] == "xg":
                xg(f[1])
            elif f[0] == "qg":
                qg(f[1])
            elif f[0] == "qw":
                qw(f[1], f[2], f[3], f[4])
            else:
                rw(f[1], f[2], f[3], f[4], f[5])

        for f in HEAD:
            if f[0] == "tt":
                ttable()
            else:
                do(f)
        for j in (1, 0, 2):
            mx_pass(0, j)
            mx_pass(1, j)
        for n in range(2):
            zexit(n)
        for n in range(2):
            mx_pass(n + 2, 1)

        NQ = N_TILES // 2
        for q in range(NQ):
            ta, tb = 2 * q, 2 * q + 1
            for f in FILL.get(q, []):
                if f[0] == "pre":
                    do(f[1:])
            if q + 1 < NQ:
                zexit(ta + 2)
                zexit(tb + 2)
            for j in (0, 2):
                fused(ta, j)
                fused(tb, j)
            for f in FILL.get(q, []):
                if f[0] == "mid":
                    do(f[1:])
            k = 2 * (q - TXQ)
            if 0 <= k < 28:
                texit("s", k)
                texit("s", k + 1)
                if k % 4 == 2:
                    store(k // 4, 0, 4)
            if q + 2 < NQ and q not in LATE_S:
                mx_pass(ta + 4, 1)
                mx_pass(tb + 4, 1)
            if q + 1 < NQ:
                for j in (0, 2):
                    mx_pass(ta + 2, j)
                    mx_pass(tb + 2, j)
            if q >= 1 and q < NQ - 1:
                tr(2 * q - 2, "t0")
                tr(2 * q - 1, "t1")
            for f in FILL.get(q, []):
                if f[0] != "pre" and f[0] != "mid":
                    do(f)
            if q + 2 < NQ and q in LATE_S:
                mx_pass(ta + 4, 1)
                mx_pass(tb + 4, 1)
        tr(28, "t0")
        tr(29, "t1")
        tr(30, "zv0")
        tr(31, "zv1")
        texit("s", 28)
        texit("v", 29)
        store(7, 0, 2)
        texit("s", 30)
        texit("v", 31)
        store(7, 2, 4)
